import numpy as np
import ml_dtypes


def mxq(x, axis, fmt="e4m3"):
    dtype, down = {"e4m3": (ml_dtypes.float8_e4m3fn, 7), "e5m2": (ml_dtypes.float8_e5m2, 14)}[fmt]
    v = np.moveaxis(np.asarray(x, np.float32).astype(ml_dtypes.bfloat16).astype(np.float64), axis, -1)
    blocks = v.reshape(v.shape[:-1] + (-1, 32))
    amax = np.abs(blocks).max(-1, keepdims=True)
    byte = np.maximum(np.where(amax > 0, np.frexp(amax)[1] - 1 + 127, 0) - down, 1)
    scale = np.exp2(byte - 127.0)
    codes = (blocks / scale).astype(np.float32).astype(dtype).astype(np.float64)
    return np.moveaxis((codes * scale).reshape(v.shape), -1, axis)


WIDE = False


def mx_kscale(k):
    if not WIDE:
        return np.ones(k)
    levels = np.array([10, -10, 5, -5, 0])
    a = np.random.permutation(np.resize(levels, k // 512 * 4)).reshape(k // 512, 4)
    idx = np.arange(k)
    return np.exp2(a[idx // 512, idx % 128 // 32])


BF16 = ml_dtypes.bfloat16


def bf(x):
    return np.asarray(x, np.float32).astype(BF16)


def f64(x):
    return np.asarray(x).astype(np.float64)


C, H, W, CO, G = 128, 64, 64, 256, 128
K = 4 * C
P = (H // 2) * (W // 2)
EPS = 1e-5


def haar_bands(x):
    xr = x.reshape(C, H // 2, 2, W // 2, 2)
    x00 = xr[:, :, 0, :, 0]
    x01 = xr[:, :, 0, :, 1]
    x10 = xr[:, :, 1, :, 0]
    x11 = xr[:, :, 1, :, 1]
    half = 0.5
    LL = (x00 + x01 + x10 + x11) * half
    HL = (-x00 - x01 + x10 + x11) * half
    LH = (-x00 + x01 - x10 + x11) * half
    HH = (x00 - x01 - x10 + x11) * half
    return LL, HL, LH, HH


def group_norm(y, scale, bias, groups):
    c, h, w = y.shape
    yg = y.reshape(groups, c // groups, h, w)
    mean = np.mean(yg, axis=(1, 2, 3), keepdims=True)
    var = np.mean(np.square(yg - mean), axis=(1, 2, 3), keepdims=True)
    yn = ((yg - mean) / np.sqrt(var + EPS)).reshape(c, h, w)
    return yn * scale[:, None, None] + bias[:, None, None]


def setup_inputs():
    s = mx_kscale(K)
    return {"x": bf(np.random.standard_normal((C, H, W))),
            "gn_scale": bf((1.0 + 0.1 * np.random.standard_normal(K)) * s),
            "gn_bias": bf(0.1 * np.random.standard_normal(K) * s),
            "w_proj": bf(np.random.standard_normal((CO, K)) / np.sqrt(K) / s[None, :])}


def reference(x, gn_scale, gn_bias, w_proj):
    LL, HL, LH, HH = haar_bands(f64(x))
    y = np.concatenate([LL, HL, LH, HH], axis=0)
    y = group_norm(y, f64(gn_scale), f64(gn_bias), G)
    z = mxq(f64(w_proj), 1, "e4m3") @ mxq(y.reshape(K, P), 0, "e4m3")
    return np.maximum(z, 0.0).reshape(CO, H // 2, W // 2)

@@ -1,0 +1,281 @@
+from contextlib import ExitStack
+
+import concourse.mybir as mybir
+from concourse.masks import make_identity
+
+F32 = mybir.dt.float32
+BF16 = mybir.dt.bfloat16
+U32 = mybir.dt.uint32
+U8 = mybir.dt.uint8
+FP8X4 = mybir.dt.float8_e4m3fn_x4
+ALU = mybir.AluOpType
+ACT = mybir.ActivationFunctionType
+AXIS = mybir.AxisListType
+
+P = 128
+H = 64
+W = 64
+BANDS = 4
+HALF_W = W // 2
+PIX = (H // 2) * HALF_W
+CO = 256
+GROUP = 4
+EPS = 1e-5
+
+LOAD_CHUNKS = 4
+CHUNK_ROWS = H // LOAD_CHUNKS
+HALVES = 2
+HALF_PIX = PIX // HALVES
+HALF_PAIRS = (H // 2) // HALVES
+M_TILES = CO // P
+RUN = 4
+
+EPS_UNHALVED = 4.0 * EPS
+
+FLOPS = 2 * CO * BANDS * P * PIX
+
+
+def tile_hwdconv_s_kernel(tc, x, gn_scale, gn_bias, w_proj, out):
+    nc = tc.nc
+    with ExitStack() as ctx:
+        keep = ctx.enter_context(tc.tile_pool(name="keep", bufs=1))
+        psum = ctx.enter_context(tc.psum_pool(name="psum", bufs=1))
+
+        x_sb = keep.tile([P, H, HALF_W, 2], BF16)
+        x_flat = x_sb[:].rearrange("p h j b -> p (h j b)")
+        x_dram = x.rearrange("c h w -> c (h w)")
+        for chunk in range(LOAD_CHUNKS):
+            cols = slice(chunk * CHUNK_ROWS * W, (chunk + 1) * CHUNK_ROWS * W)
+            nc.sync.dma_start(out=x_flat[:, cols], in_=x_dram[:, cols])
+        w_sb = keep.tile([P, M_TILES, BANDS, P], BF16)
+        nc.sync.dma_start(
+            out=w_sb[:], in_=w_proj.rearrange("(m o) (t c) -> o m t c", o=P, c=P)
+        )
+        gn_rows = keep.tile([P, P], BF16)
+        nc.vector.memset(gn_rows[:], 0.0)
+        nc.scalar.dma_start(
+            out=gn_rows[0:BANDS, :], in_=gn_scale.rearrange("(t c) -> t c", c=P)
+        )
+        nc.scalar.dma_start(
+            out=gn_rows[BANDS : 2 * BANDS, :], in_=gn_bias.rearrange("(t c) -> t c", c=P)
+        )
+
+        one = keep.tile([P, 1], F32)
+        nc.vector.memset(one[:], 1.0)
+        table_warm = keep.tile([P, 1], F32)
+        nc.scalar.activation(out=table_warm[:], in_=one[:], func=ACT.Sqrt)
+
+        ident = keep.tile([P, P], BF16)
+        make_identity(nc, ident[:])
+        same_group = keep.tile([P, P // GROUP], F32)
+        nc.vector.tensor_reduce(
+            out=same_group[:],
+            in_=ident[:].rearrange("p (g j) -> p g j", j=GROUP),
+            axis=AXIS.X,
+            op=ALU.add,
+        )
+        group_avg = keep.tile([P, P // GROUP, GROUP], F32)
+        nc.vector.tensor_scalar(
+            out=group_avg[:],
+            in0=same_group[:].unsqueeze(2).to_broadcast([P, P // GROUP, GROUP]),
+            scalar1=1.0 / (GROUP * PIX),
+            scalar2=None,
+            op0=ALU.mult,
+        )
+        group_avg_2d = group_avg[:].rearrange("p g j -> p (g j)")
+
+        gain_pull = keep.tile([P, 2, 2 * BANDS], F32)
+        gn_bias_sb = keep.tile([P, BANDS], F32)
+        gn_t = psum.tile([P, P], BF16, tag="tiny")
+        nc.tensor.transpose(gn_t[:], gn_rows[:], ident[:])
+        nc.scalar.copy(out=gain_pull[:, 0, 0:BANDS], in_=gn_t[:, 0:BANDS])
+        nc.scalar.copy(out=gn_bias_sb[:], in_=gn_t[:, BANDS : 2 * BANDS])
+
+        row_sum = keep.tile([P, H, HALF_W], F32)
+        row_diff = keep.tile([P, H, HALF_W], F32)
+        for chunk in range(LOAD_CHUNKS):
+            rows = slice(chunk * CHUNK_ROWS, (chunk + 1) * CHUNK_ROWS)
+            left, right = x_sb[:, rows, :, 0], x_sb[:, rows, :, 1]
+            nc.vector.tensor_tensor(out=row_sum[:, rows, :], in0=left, in1=right, op=ALU.add)
+            nc.vector.tensor_tensor(
+                out=row_diff[:, rows, :], in0=right, in1=left, op=ALU.subtract
+            )
+        paired = [
+            src[:].rearrange("p (i a) j -> p i a j", a=2) for src in (row_sum, row_diff)
+        ]
+
+        est_pairs = CHUNK_ROWS // 2
+        est_scrap = keep.tile([P, 2, 2, est_pairs, HALF_W], BF16)
+        est_rows = keep.tile([P, 2, 2], F32)
+        for a in range(2):
+            for k in range(2):
+                nc.scalar.activation(
+                    out=est_scrap[:, a, k, :, :],
+                    in_=paired[k][:, 0:est_pairs, a, :],
+                    func=ACT.Copy,
+                    accum_out=est_rows[:, a, k : k + 1],
+                )
+        est_bands = keep.tile([P, 2, 2], F32)
+        nc.vector.tensor_tensor(
+            out=est_bands[:, :, 0], in0=est_rows[:, 0, :], in1=est_rows[:, 1, :], op=ALU.add
+        )
+        nc.vector.tensor_tensor(
+            out=est_bands[:, :, 1], in0=est_rows[:, 1, :], in1=est_rows[:, 0, :], op=ALU.subtract
+        )
+        shift_ps = psum.tile([P, BANDS], F32, tag="tiny")
+        nc.tensor.matmul(
+            out=shift_ps[:],
+            lhsT=group_avg_2d,
+            rhs=est_bands[:].rearrange("p k c -> p (k c)"),
+            start=True,
+            stop=True,
+        )
+        shift = keep.tile([P, BANDS], F32)
+        nc.scalar.mul(out=shift[:], in_=shift_ps[:], mul=float(LOAD_CHUNKS))
+
+        w_t = psum.tile([P, M_TILES, BANDS, P], BF16)
+        for m in range(M_TILES):
+            for t in range(BANDS):
+                nc.tensor.transpose(w_t[:, m, t, :], w_sb[:, m, t, :], ident[:])
+        w_grouped = keep.tile([P, M_TILES, P, BANDS], BF16, align_bytes=64)
+        nc.scalar.copy(out=w_grouped[:], in_=w_t[:].rearrange("p m t o -> p m o t"))
+        w_codes = keep.tile([P, CO], U32, align_bytes=64)
+        w_scales = keep.tile([P, CO], U8, align_bytes=64)
+
+        bands = keep.tile([P, BANDS, PIX], F32)
+        squares_scrap = keep.tile([P, HALVES, BANDS, HALF_PIX], BF16)
+        sums = keep.tile([P, HALVES, BANDS], F32)
+        sumsq = keep.tile([P, HALVES, BANDS], F32)
+        mean_ps = psum.tile([P, BANDS], F32)
+        meansq_ps = psum.tile([P, BANDS], F32)
+        for half in range(HALVES):
+            px = slice(half * HALF_PIX, (half + 1) * HALF_PIX)
+            pairs = slice(half * HALF_PAIRS, (half + 1) * HALF_PAIRS)
+            for t in range(BANDS):
+                upper = paired[t // 2][:, pairs, 0, :]
+                lower = paired[t // 2][:, pairs, 1, :]
+                first, second, combine = (
+                    (lower, upper, ALU.subtract) if t % 2 else (upper, lower, ALU.add)
+                )
+                nc.vector.scalar_tensor_tensor(
+                    out=bands[:, t, px].rearrange("p (i j) -> p i j", j=HALF_W),
+                    in0=first,
+                    scalar=shift[:, t : t + 1],
+                    in1=second,
+                    op0=ALU.subtract,
+                    op1=combine,
+                    accum_out=sums[:, half, t : t + 1],
+                )
+                nc.scalar.activation(
+                    out=squares_scrap[:, half, t, :],
+                    in_=bands[:, t, px],
+                    func=ACT.Square,
+                    accum_out=sumsq[:, half, t : t + 1],
+                )
+            first_half, last_half = half == 0, half == HALVES - 1
+            nc.tensor.matmul(
+                out=mean_ps[:], lhsT=group_avg_2d, rhs=sums[:, half, :],
+                start=first_half, stop=last_half,
+            )
+            nc.tensor.matmul(
+                out=meansq_ps[:], lhsT=group_avg_2d, rhs=sumsq[:, half, :],
+                start=first_half, stop=last_half,
+            )
+
+        nc.vector.quantize_mx(
+            out=w_codes[:].bitcast(FP8X4),
+            scales=w_scales[:],
+            in_=w_grouped[:].rearrange("p m o t -> p (m o t)"),
+        )
+
+        mean = keep.tile([P, BANDS], F32)
+        nc.vector.tensor_copy(out=mean[:], in_=mean_ps[:])
+        mean_squared = keep.tile([P, BANDS], F32)
+        nc.vector.tensor_tensor(out=mean_squared[:], in0=mean_ps[:], in1=mean[:], op=ALU.mult)
+        nc.vector.scalar_tensor_tensor(
+            out=gain_pull[:, 1, 0:BANDS],
+            in0=mean[:],
+            scalar=-1.0,
+            in1=gain_pull[:, 0, 0:BANDS],
+            op0=ALU.mult,
+            op1=ALU.mult,
+        )
+        var_eps = keep.tile([P, BANDS], F32)
+        nc.vector.scalar_tensor_tensor(
+            out=var_eps[:],
+            in0=meansq_ps[:],
+            scalar=EPS_UNHALVED,
+            in1=mean_squared[:],
+            op0=ALU.add,
+            op1=ALU.subtract,
+        )
+        std = keep.tile([P, BANDS], F32)
+        nc.scalar.activation(out=std[:], in_=var_eps[:], func=ACT.Sqrt)
+        rstd = keep.tile([P, BANDS], F32)
+        nc.vector.reciprocal(out=rstd[:], in_=std[:])
+        slope_pull = keep.tile([P, 2, BANDS], F32)
+        nc.vector.tensor_tensor(
+            out=slope_pull[:],
+            in0=gain_pull[:, :, 0:BANDS],
+            in1=rstd[:].unsqueeze(1).to_broadcast([P, 2, BANDS]),
+            op=ALU.mult,
+        )
+        offset = keep.tile([P, BANDS], F32)
+        nc.vector.tensor_tensor(
+            out=offset[:], in0=slope_pull[:, 1, :], in1=gn_bias_sb[:], op=ALU.add
+        )
+
+        y_planar = keep.tile([P, BANDS, PIX], BF16)
+        for half in range(HALVES):
+            px = slice(half * HALF_PIX, (half + 1) * HALF_PIX)
+            for t in range(BANDS):
+                slope_t, offset_t = slope_pull[:, 0, t : t + 1], offset[:, t : t + 1]
+                if t % 2 == 0:
+                    nc.scalar.activation(
+                        out=y_planar[:, t, px], in_=bands[:, t, px],
+                        func=ACT.Identity, scale=slope_t, bias=offset_t,
+                    )
+                else:
+                    nc.vector.tensor_scalar(
+                        out=y_planar[:, t, px], in0=bands[:, t, px],
+                        scalar1=slope_t, scalar2=offset_t, op0=ALU.mult, op1=ALU.add,
+                    )
+
+        y_grouped = keep.tile([P, PIX, BANDS], BF16, align_bytes=64)
+        y_codes = keep.tile([P, PIX], U32, align_bytes=64)
+        y_scales = keep.tile([P, PIX], U8, align_bytes=64)
+        for half in range(HALVES):
+            px = slice(half * HALF_PIX, (half + 1) * HALF_PIX)
+            nc.vector.tensor_copy(
+                out=y_grouped[:, px, :].rearrange("p (n r) t -> p n t r", r=RUN),
+                in_=y_planar[:, :, px].rearrange("p t (n r) -> p n t r", r=RUN),
+            )
+        for half in range(HALVES):
+            px = slice(half * HALF_PIX, (half + 1) * HALF_PIX)
+            nc.vector.quantize_mx(
+                out=y_codes[:, px].bitcast(FP8X4),
+                scales=y_scales[:, px],
+                in_=y_grouped[:, px, :].rearrange("p n t -> p (n t)"),
+            )
+
+        out_dram = out.rearrange("(m o) i j -> m o (i j)", o=P)
+        for half in range(HALVES):
+            px = slice(half * HALF_PIX, (half + 1) * HALF_PIX)
+            for m in range(M_TILES):
+                o_cols = slice(m * P, (m + 1) * P)
+                acc = psum.tile([P, HALF_PIX], F32, name="acc%d%d" % (half, m))
+                nc.tensor.matmul_mx(
+                    out=acc[:],
+                    lhsT=w_codes[:, o_cols].bitcast(FP8X4),
+                    lhsT_scale=w_scales[:, o_cols],
+                    rhs=y_codes[:, px].bitcast(FP8X4),
+                    rhs_scale=y_scales[:, px],
+                    start=True,
+                    stop=True,
+                )
+                result = keep.tile([P, HALF_PIX], F32, name="result%d%d" % (half, m))
+                if m % 2 == 0:
+                    nc.scalar.activation(out=result[:], in_=acc[:], func=ACT.Relu)
+                else:
+                    nc.vector.tensor_scalar_max(out=result[:], in0=acc[:], scalar1=0.0)
+                nc.sync.dma_start(out=out_dram[m][:, px], in_=result[:])

@@ -27,6 +27,8 @@ CHUNK_ROWS = H // LOAD_CHUNKS
 HALVES = 2
 HALF_PIX = PIX // HALVES
 HALF_PAIRS = (H // 2) // HALVES
+N_TILES = 4
+N_PIX = PIX // N_TILES
 M_TILES = CO // P
 RUN = 4
 
@@ -40,17 +42,20 @@ def tile_hwdconv_s_kernel(tc, x, gn_scale, gn_bias, w_proj, out):
     with ExitStack() as ctx:
         keep = ctx.enter_context(tc.tile_pool(name="keep", bufs=1))
         psum = ctx.enter_context(tc.psum_pool(name="psum", bufs=1))
+        acc_pool = ctx.enter_context(tc.psum_pool(name="acc_pool", bufs=4))
+        ctx.enter_context(tc.manual_schedule())
 
         x_sb = keep.tile([P, H, HALF_W, 2], BF16)
         x_flat = x_sb[:].rearrange("p h j b -> p (h j b)")
         x_dram = x.rearrange("c h w -> c (h w)")
+        w_sb = keep.tile([P, M_TILES, BANDS, P], BF16)
         for chunk in range(LOAD_CHUNKS):
             cols = slice(chunk * CHUNK_ROWS * W, (chunk + 1) * CHUNK_ROWS * W)
             nc.sync.dma_start(out=x_flat[:, cols], in_=x_dram[:, cols])
-        w_sb = keep.tile([P, M_TILES, BANDS, P], BF16)
-        nc.sync.dma_start(
-            out=w_sb[:], in_=w_proj.rearrange("(m o) (t c) -> o m t c", o=P, c=P)
-        )
+            if chunk == 1:
+                nc.sync.dma_start(
+                    out=w_sb[:], in_=w_proj.rearrange("(m o) (t c) -> o m t c", o=P, c=P)
+                )
         gn_rows = keep.tile([P, P], BF16)
         nc.vector.memset(gn_rows[:], 0.0)
         nc.scalar.dma_start(
@@ -84,26 +89,21 @@ def tile_hwdconv_s_kernel(tc, x, gn_scale, gn_bias, w_proj, out):
         )
         group_avg_2d = group_avg[:].rearrange("p g j -> p (g j)")
 
-        gain_pull = keep.tile([P, 2, 2 * BANDS], F32)
-        gn_bias_sb = keep.tile([P, BANDS], F32)
-        gn_t = psum.tile([P, P], BF16, tag="tiny")
-        nc.tensor.transpose(gn_t[:], gn_rows[:], ident[:])
-        nc.scalar.copy(out=gain_pull[:, 0, 0:BANDS], in_=gn_t[:, 0:BANDS])
-        nc.scalar.copy(out=gn_bias_sb[:], in_=gn_t[:, BANDS : 2 * BANDS])
-
         row_sum = keep.tile([P, H, HALF_W], F32)
         row_diff = keep.tile([P, H, HALF_W], F32)
-        for chunk in range(LOAD_CHUNKS):
+        paired = [
+            src[:].rearrange("p (i a) j -> p i a j", a=2) for src in (row_sum, row_diff)
+        ]
+
+        def haar_along_rows(chunk):
             rows = slice(chunk * CHUNK_ROWS, (chunk + 1) * CHUNK_ROWS)
             left, right = x_sb[:, rows, :, 0], x_sb[:, rows, :, 1]
             nc.vector.tensor_tensor(out=row_sum[:, rows, :], in0=left, in1=right, op=ALU.add)
             nc.vector.tensor_tensor(
                 out=row_diff[:, rows, :], in0=right, in1=left, op=ALU.subtract
             )
-        paired = [
-            src[:].rearrange("p (i a) j -> p i a j", a=2) for src in (row_sum, row_diff)
-        ]
 
+        haar_along_rows(0)
         est_pairs = CHUNK_ROWS // 2
         est_scrap = keep.tile([P, 2, 2, est_pairs, HALF_W], BF16)
         est_rows = keep.tile([P, 2, 2], F32)
@@ -115,6 +115,8 @@ def tile_hwdconv_s_kernel(tc, x, gn_scale, gn_bias, w_proj, out):
                     func=ACT.Copy,
                     accum_out=est_rows[:, a, k : k + 1],
                 )
+        haar_along_rows(1)
+        haar_along_rows(2)
         est_bands = keep.tile([P, 2, 2], F32)
         nc.vector.tensor_tensor(
             out=est_bands[:, :, 0], in0=est_rows[:, 0, :], in1=est_rows[:, 1, :], op=ALU.add
@@ -122,7 +124,22 @@ def tile_hwdconv_s_kernel(tc, x, gn_scale, gn_bias, w_proj, out):
         nc.vector.tensor_tensor(
             out=est_bands[:, :, 1], in0=est_rows[:, 1, :], in1=est_rows[:, 0, :], op=ALU.subtract
         )
-        shift_ps = psum.tile([P, BANDS], F32, tag="tiny")
+        haar_along_rows(3)
+
+        gn_t = psum.tile([P, P], BF16)
+        nc.tensor.transpose(gn_t[:], gn_rows[:], ident[:])
+        w_t = psum.tile([P, M_TILES, BANDS, P], BF16)
+        for m in range(M_TILES):
+            for t in range(BANDS):
+                nc.tensor.transpose(w_t[:, m, t, :], w_sb[:, m, t, :], ident[:])
+        w_grouped = keep.tile([P, M_TILES, P, BANDS], BF16, align_bytes=64)
+        nc.scalar.copy(out=w_grouped[:], in_=w_t[:].rearrange("p m t o -> p m o t"))
+        gain_pull = keep.tile([P, 2, 2 * BANDS], F32)
+        gn_bias_sb = keep.tile([P, BANDS], F32)
+        nc.scalar.copy(out=gain_pull[:, 0, 0:BANDS], in_=gn_t[:, 0:BANDS])
+        nc.scalar.copy(out=gn_bias_sb[:], in_=gn_t[:, BANDS : 2 * BANDS])
+
+        shift_ps = psum.tile([P, BANDS], F32, tag="mean")
         nc.tensor.matmul(
             out=shift_ps[:],
             lhsT=group_avg_2d,
@@ -133,20 +150,11 @@ def tile_hwdconv_s_kernel(tc, x, gn_scale, gn_bias, w_proj, out):
         shift = keep.tile([P, BANDS], F32)
         nc.scalar.mul(out=shift[:], in_=shift_ps[:], mul=float(LOAD_CHUNKS))
 
-        w_t = psum.tile([P, M_TILES, BANDS, P], BF16)
-        for m in range(M_TILES):
-            for t in range(BANDS):
-                nc.tensor.transpose(w_t[:, m, t, :], w_sb[:, m, t, :], ident[:])
-        w_grouped = keep.tile([P, M_TILES, P, BANDS], BF16, align_bytes=64)
-        nc.scalar.copy(out=w_grouped[:], in_=w_t[:].rearrange("p m t o -> p m o t"))
-        w_codes = keep.tile([P, CO], U32, align_bytes=64)
-        w_scales = keep.tile([P, CO], U8, align_bytes=64)
-
         bands = keep.tile([P, BANDS, PIX], F32)
         squares_scrap = keep.tile([P, HALVES, BANDS, HALF_PIX], BF16)
         sums = keep.tile([P, HALVES, BANDS], F32)
         sumsq = keep.tile([P, HALVES, BANDS], F32)
-        mean_ps = psum.tile([P, BANDS], F32)
+        mean_ps = psum.tile([P, BANDS], F32, tag="mean")
         meansq_ps = psum.tile([P, BANDS], F32)
         for half in range(HALVES):
             px = slice(half * HALF_PIX, (half + 1) * HALF_PIX)
@@ -182,6 +190,8 @@ def tile_hwdconv_s_kernel(tc, x, gn_scale, gn_bias, w_proj, out):
                 start=first_half, stop=last_half,
             )
 
+        w_codes = keep.tile([P, CO], U32, align_bytes=64)
+        w_scales = keep.tile([P, CO], U8, align_bytes=64)
         nc.vector.quantize_mx(
             out=w_codes[:].bitcast(FP8X4),
             scales=w_scales[:],
@@ -226,8 +236,8 @@ def tile_hwdconv_s_kernel(tc, x, gn_scale, gn_bias, w_proj, out):
         )
 
         y_planar = keep.tile([P, BANDS, PIX], BF16)
-        for half in range(HALVES):
-            px = slice(half * HALF_PIX, (half + 1) * HALF_PIX)
+        for n in range(N_TILES):
+            px = slice(n * N_PIX, (n + 1) * N_PIX)
             for t in range(BANDS):
                 slope_t, offset_t = slope_pull[:, 0, t : t + 1], offset[:, t : t + 1]
                 if t % 2 == 0:
@@ -244,26 +254,28 @@ def tile_hwdconv_s_kernel(tc, x, gn_scale, gn_bias, w_proj, out):
         y_grouped = keep.tile([P, PIX, BANDS], BF16, align_bytes=64)
         y_codes = keep.tile([P, PIX], U32, align_bytes=64)
         y_scales = keep.tile([P, PIX], U8, align_bytes=64)
-        for half in range(HALVES):
-            px = slice(half * HALF_PIX, (half + 1) * HALF_PIX)
+        out_dram = out.rearrange("(m o) i j -> m o (i j)", o=P)
+
+        def regroup(n):
+            px = slice(n * N_PIX, (n + 1) * N_PIX)
             nc.vector.tensor_copy(
-                out=y_grouped[:, px, :].rearrange("p (n r) t -> p n t r", r=RUN),
-                in_=y_planar[:, :, px].rearrange("p t (n r) -> p n t r", r=RUN),
+                out=y_grouped[:, px, :].rearrange("p (c r) t -> p c t r", r=RUN),
+                in_=y_planar[:, :, px].rearrange("p t (c r) -> p c t r", r=RUN),
             )
-        for half in range(HALVES):
-            px = slice(half * HALF_PIX, (half + 1) * HALF_PIX)
+
+        regroup(0)
+        for n in range(N_TILES):
+            px = slice(n * N_PIX, (n + 1) * N_PIX)
+            if n + 1 < N_TILES:
+                regroup(n + 1)
             nc.vector.quantize_mx(
                 out=y_codes[:, px].bitcast(FP8X4),
                 scales=y_scales[:, px],
-                in_=y_grouped[:, px, :].rearrange("p n t -> p (n t)"),
+                in_=y_grouped[:, px, :].rearrange("p c t -> p (c t)"),
             )
-
-        out_dram = out.rearrange("(m o) i j -> m o (i j)", o=P)
-        for half in range(HALVES):
-            px = slice(half * HALF_PIX, (half + 1) * HALF_PIX)
             for m in range(M_TILES):
                 o_cols = slice(m * P, (m + 1) * P)
-                acc = psum.tile([P, HALF_PIX], F32, name="acc%d%d" % (half, m))
+                acc = acc_pool.tile([P, N_PIX], F32)
                 nc.tensor.matmul_mx(
                     out=acc[:],
                     lhsT=w_codes[:, o_cols].bitcast(FP8X4),
@@ -273,9 +285,9 @@ def tile_hwdconv_s_kernel(tc, x, gn_scale, gn_bias, w_proj, out):
                     start=True,
                     stop=True,
                 )
-                result = keep.tile([P, HALF_PIX], F32, name="result%d%d" % (half, m))
-                if m % 2 == 0:
-                    nc.scalar.activation(out=result[:], in_=acc[:], func=ACT.Relu)
-                else:
+                result = keep.tile([P, N_PIX], F32, name="result%d%d" % (n, m))
+                if n == N_TILES - 1 and m == M_TILES - 1:
                     nc.vector.tensor_scalar_max(out=result[:], in0=acc[:], scalar1=0.0)
+                else:
+                    nc.scalar.activation(out=result[:], in_=acc[:], func=ACT.Relu)
                 nc.sync.dma_start(out=out_dram[m][:, px], in_=result[:])

@@ -22,8 +22,9 @@ CO = 256
 GROUP = 4
 EPS = 1e-5
 
-LOAD_CHUNKS = 4
-CHUNK_ROWS = H // LOAD_CHUNKS
+FIRST_CHUNK_ROWS = 4
+MAX_CHUNK_ROWS = 16
+EST_ROWS = 16
 HALVES = 2
 HALF_PIX = PIX // HALVES
 HALF_PAIRS = (H // 2) // HALVES
@@ -49,19 +50,20 @@ def tile_hwdconv_s_kernel(tc, x, gn_scale, gn_bias, w_proj, out):
         x_flat = x_sb[:].rearrange("p h j b -> p (h j b)")
         x_dram = x.rearrange("c h w -> c (h w)")
         w_sb = keep.tile([P, M_TILES, BANDS, P], BF16)
-        for chunk in range(LOAD_CHUNKS):
-            cols = slice(chunk * CHUNK_ROWS * W, (chunk + 1) * CHUNK_ROWS * W)
-            nc.sync.dma_start(out=x_flat[:, cols], in_=x_dram[:, cols])
-            if chunk == 1:
+        bounds = [0]
+        while bounds[-1] < H:
+            bounds.append(bounds[-1] + min(max(bounds[-1], FIRST_CHUNK_ROWS), MAX_CHUNK_ROWS))
+        chunks = list(zip(bounds[:-1], bounds[1:]))
+        for row0, row1 in chunks:
+            nc.sync.dma_start(out=x_flat[:, row0 * W : row1 * W], in_=x_dram[:, row0 * W : row1 * W])
+            if row1 == H // 2:
                 nc.sync.dma_start(
                     out=w_sb[:], in_=w_proj.rearrange("(m o) (t c) -> o m t c", o=P, c=P)
                 )
         gn_rows = keep.tile([P, P], BF16)
         nc.vector.memset(gn_rows[:], 0.0)
-        nc.scalar.dma_start(
-            out=gn_rows[0:BANDS, :], in_=gn_scale.rearrange("(t c) -> t c", c=P)
-        )
-        nc.scalar.dma_start(
+        nc.sync.dma_start(out=gn_rows[0:BANDS, :], in_=gn_scale.rearrange("(t c) -> t c", c=P))
+        nc.sync.dma_start(
             out=gn_rows[BANDS : 2 * BANDS, :], in_=gn_bias.rearrange("(t c) -> t c", c=P)
         )
 
@@ -95,16 +97,18 @@ def tile_hwdconv_s_kernel(tc, x, gn_scale, gn_bias, w_proj, out):
             src[:].rearrange("p (i a) j -> p i a j", a=2) for src in (row_sum, row_diff)
         ]
 
-        def haar_along_rows(chunk):
-            rows = slice(chunk * CHUNK_ROWS, (chunk + 1) * CHUNK_ROWS)
+        def haar_along_rows(row0, row1):
+            rows = slice(row0, row1)
             left, right = x_sb[:, rows, :, 0], x_sb[:, rows, :, 1]
             nc.vector.tensor_tensor(out=row_sum[:, rows, :], in0=left, in1=right, op=ALU.add)
             nc.vector.tensor_tensor(
                 out=row_diff[:, rows, :], in0=right, in1=left, op=ALU.subtract
             )
 
-        haar_along_rows(0)
-        est_pairs = CHUNK_ROWS // 2
+        for row0, row1 in chunks:
+            if row1 <= EST_ROWS:
+                haar_along_rows(row0, row1)
+        est_pairs = EST_ROWS // 2
         est_scrap = keep.tile([P, 2, 2, est_pairs, HALF_W], BF16)
         est_rows = keep.tile([P, 2, 2], F32)
         for a in range(2):
@@ -115,8 +119,9 @@ def tile_hwdconv_s_kernel(tc, x, gn_scale, gn_bias, w_proj, out):
                     func=ACT.Copy,
                     accum_out=est_rows[:, a, k : k + 1],
                 )
-        haar_along_rows(1)
-        haar_along_rows(2)
+        for row0, row1 in chunks:
+            if EST_ROWS < row1 < H:
+                haar_along_rows(row0, row1)
         est_bands = keep.tile([P, 2, 2], F32)
         nc.vector.tensor_tensor(
             out=est_bands[:, :, 0], in0=est_rows[:, 0, :], in1=est_rows[:, 1, :], op=ALU.add
@@ -124,20 +129,14 @@ def tile_hwdconv_s_kernel(tc, x, gn_scale, gn_bias, w_proj, out):
         nc.vector.tensor_tensor(
             out=est_bands[:, :, 1], in0=est_rows[:, 1, :], in1=est_rows[:, 0, :], op=ALU.subtract
         )
-        haar_along_rows(3)
+        haar_along_rows(bounds[-2], bounds[-1])
 
-        gn_t = psum.tile([P, P], BF16)
-        nc.tensor.transpose(gn_t[:], gn_rows[:], ident[:])
         w_t = psum.tile([P, M_TILES, BANDS, P], BF16)
         for m in range(M_TILES):
             for t in range(BANDS):
                 nc.tensor.transpose(w_t[:, m, t, :], w_sb[:, m, t, :], ident[:])
         w_grouped = keep.tile([P, M_TILES, P, BANDS], BF16, align_bytes=64)
         nc.scalar.copy(out=w_grouped[:], in_=w_t[:].rearrange("p m t o -> p m o t"))
-        gain_pull = keep.tile([P, 2, 2 * BANDS], F32)
-        gn_bias_sb = keep.tile([P, BANDS], F32)
-        nc.scalar.copy(out=gain_pull[:, 0, 0:BANDS], in_=gn_t[:, 0:BANDS])
-        nc.scalar.copy(out=gn_bias_sb[:], in_=gn_t[:, BANDS : 2 * BANDS])
 
         shift_ps = psum.tile([P, BANDS], F32, tag="mean")
         nc.tensor.matmul(
@@ -148,7 +147,14 @@ def tile_hwdconv_s_kernel(tc, x, gn_scale, gn_bias, w_proj, out):
             stop=True,
         )
         shift = keep.tile([P, BANDS], F32)
-        nc.scalar.mul(out=shift[:], in_=shift_ps[:], mul=float(LOAD_CHUNKS))
+        nc.scalar.mul(out=shift[:], in_=shift_ps[:], mul=float(H // EST_ROWS))
+
+        gn_t = psum.tile([P, P], BF16)
+        nc.tensor.transpose(gn_t[:], gn_rows[:], ident[:])
+        gain_pull = keep.tile([P, 2, 2 * BANDS], F32)
+        gn_bias_sb = keep.tile([P, BANDS], F32)
+        nc.scalar.copy(out=gain_pull[:, 0, 0:BANDS], in_=gn_t[:, 0:BANDS])
+        nc.scalar.copy(out=gn_bias_sb[:], in_=gn_t[:, BANDS : 2 * BANDS])
 
         bands = keep.tile([P, BANDS, PIX], F32)
         squares_scrap = keep.tile([P, HALVES, BANDS, HALF_PIX], BF16)

@@ -24,7 +24,7 @@ EPS = 1e-5
 
 FIRST_CHUNK_ROWS = 4
 MAX_CHUNK_ROWS = 16
-EST_ROWS = 16
+EST_ROWS = 8
 HALVES = 2
 HALF_PIX = PIX // HALVES
 HALF_PAIRS = (H // 2) // HALVES

from contextlib import ExitStack

import concourse.mybir as mybir
from concourse.masks import make_identity

F32 = mybir.dt.float32
BF16 = mybir.dt.bfloat16
U32 = mybir.dt.uint32
U8 = mybir.dt.uint8
FP8X4 = mybir.dt.float8_e4m3fn_x4
ALU = mybir.AluOpType
ACT = mybir.ActivationFunctionType
AXIS = mybir.AxisListType

P = 128
H = 64
W = 64
BANDS = 4
HALF_W = W // 2
PIX = (H // 2) * HALF_W
CO = 256
GROUP = 4
EPS = 1e-5

FIRST_CHUNK_ROWS = 4
MAX_CHUNK_ROWS = 16
EST_ROWS = 8
HALVES = 2
HALF_PIX = PIX // HALVES
HALF_PAIRS = (H // 2) // HALVES
N_TILES = 4
N_PIX = PIX // N_TILES
M_TILES = CO // P
RUN = 4

EPS_UNHALVED = 4.0 * EPS

FLOPS = 2 * CO * BANDS * P * PIX


def tile_hwdconv_s_kernel(tc, x, gn_scale, gn_bias, w_proj, out):
    nc = tc.nc
    with ExitStack() as ctx:
        keep = ctx.enter_context(tc.tile_pool(name="keep", bufs=1))
        psum = ctx.enter_context(tc.psum_pool(name="psum", bufs=1))
        acc_pool = ctx.enter_context(tc.psum_pool(name="acc_pool", bufs=4))
        ctx.enter_context(tc.manual_schedule())

        x_sb = keep.tile([P, H, HALF_W, 2], BF16)
        x_flat = x_sb[:].rearrange("p h j b -> p (h j b)")
        x_dram = x.rearrange("c h w -> c (h w)")
        w_sb = keep.tile([P, M_TILES, BANDS, P], BF16)
        bounds = [0]
        while bounds[-1] < H:
            bounds.append(bounds[-1] + min(max(bounds[-1], FIRST_CHUNK_ROWS), MAX_CHUNK_ROWS))
        chunks = list(zip(bounds[:-1], bounds[1:]))
        for row0, row1 in chunks:
            nc.sync.dma_start(out=x_flat[:, row0 * W : row1 * W], in_=x_dram[:, row0 * W : row1 * W])
            if row1 == H // 2:
                nc.sync.dma_start(
                    out=w_sb[:], in_=w_proj.rearrange("(m o) (t c) -> o m t c", o=P, c=P)
                )
        gn_rows = keep.tile([P, P], BF16)
        nc.vector.memset(gn_rows[:], 0.0)
        nc.sync.dma_start(out=gn_rows[0:BANDS, :], in_=gn_scale.rearrange("(t c) -> t c", c=P))
        nc.sync.dma_start(
            out=gn_rows[BANDS : 2 * BANDS, :], in_=gn_bias.rearrange("(t c) -> t c", c=P)
        )

        one = keep.tile([P, 1], F32)
        nc.vector.memset(one[:], 1.0)
        table_warm = keep.tile([P, 1], F32)
        nc.scalar.activation(out=table_warm[:], in_=one[:], func=ACT.Sqrt)

        ident = keep.tile([P, P], BF16)
        make_identity(nc, ident[:])
        same_group = keep.tile([P, P // GROUP], F32)
        nc.vector.tensor_reduce(
            out=same_group[:],
            in_=ident[:].rearrange("p (g j) -> p g j", j=GROUP),
            axis=AXIS.X,
            op=ALU.add,
        )
        group_avg = keep.tile([P, P // GROUP, GROUP], F32)
        nc.vector.tensor_scalar(
            out=group_avg[:],
            in0=same_group[:].unsqueeze(2).to_broadcast([P, P // GROUP, GROUP]),
            scalar1=1.0 / (GROUP * PIX),
            scalar2=None,
            op0=ALU.mult,
        )
        group_avg_2d = group_avg[:].rearrange("p g j -> p (g j)")

        row_sum = keep.tile([P, H, HALF_W], F32)
        row_diff = keep.tile([P, H, HALF_W], F32)
        paired = [
            src[:].rearrange("p (i a) j -> p i a j", a=2) for src in (row_sum, row_diff)
        ]

        def haar_along_rows(row0, row1):
            rows = slice(row0, row1)
            left, right = x_sb[:, rows, :, 0], x_sb[:, rows, :, 1]
            nc.vector.tensor_tensor(out=row_sum[:, rows, :], in0=left, in1=right, op=ALU.add)
            nc.vector.tensor_tensor(
                out=row_diff[:, rows, :], in0=right, in1=left, op=ALU.subtract
            )

        for row0, row1 in chunks:
            if row1 <= EST_ROWS:
                haar_along_rows(row0, row1)
        est_pairs = EST_ROWS // 2
        est_scrap = keep.tile([P, 2, 2, est_pairs, HALF_W], BF16)
        est_rows = keep.tile([P, 2, 2], F32)
        for a in range(2):
            for k in range(2):
                nc.scalar.activation(
                    out=est_scrap[:, a, k, :, :],
                    in_=paired[k][:, 0:est_pairs, a, :],
                    func=ACT.Copy,
                    accum_out=est_rows[:, a, k : k + 1],
                )
        for row0, row1 in chunks:
            if EST_ROWS < row1 < H:
                haar_along_rows(row0, row1)
        est_bands = keep.tile([P, 2, 2], F32)
        nc.vector.tensor_tensor(
            out=est_bands[:, :, 0], in0=est_rows[:, 0, :], in1=est_rows[:, 1, :], op=ALU.add
        )
        nc.vector.tensor_tensor(
            out=est_bands[:, :, 1], in0=est_rows[:, 1, :], in1=est_rows[:, 0, :], op=ALU.subtract
        )
        haar_along_rows(bounds[-2], bounds[-1])

        w_t = psum.tile([P, M_TILES, BANDS, P], BF16)
        for m in range(M_TILES):
            for t in range(BANDS):
                nc.tensor.transpose(w_t[:, m, t, :], w_sb[:, m, t, :], ident[:])
        w_grouped = keep.tile([P, M_TILES, P, BANDS], BF16, align_bytes=64)
        nc.scalar.copy(out=w_grouped[:], in_=w_t[:].rearrange("p m t o -> p m o t"))

        shift_ps = psum.tile([P, BANDS], F32, tag="mean")
        nc.tensor.matmul(
            out=shift_ps[:],
            lhsT=group_avg_2d,
            rhs=est_bands[:].rearrange("p k c -> p (k c)"),
            start=True,
            stop=True,
        )
        shift = keep.tile([P, BANDS], F32)
        nc.scalar.mul(out=shift[:], in_=shift_ps[:], mul=float(H // EST_ROWS))

        gn_t = psum.tile([P, P], BF16)
        nc.tensor.transpose(gn_t[:], gn_rows[:], ident[:])
        gain_pull = keep.tile([P, 2, 2 * BANDS], F32)
        gn_bias_sb = keep.tile([P, BANDS], F32)
        nc.scalar.copy(out=gain_pull[:, 0, 0:BANDS], in_=gn_t[:, 0:BANDS])
        nc.scalar.copy(out=gn_bias_sb[:], in_=gn_t[:, BANDS : 2 * BANDS])

        bands = keep.tile([P, BANDS, PIX], F32)
        squares_scrap = keep.tile([P, HALVES, BANDS, HALF_PIX], BF16)
        sums = keep.tile([P, HALVES, BANDS], F32)
        sumsq = keep.tile([P, HALVES, BANDS], F32)
        mean_ps = psum.tile([P, BANDS], F32, tag="mean")
        meansq_ps = psum.tile([P, BANDS], F32)
        for half in range(HALVES):
            px = slice(half * HALF_PIX, (half + 1) * HALF_PIX)
            pairs = slice(half * HALF_PAIRS, (half + 1) * HALF_PAIRS)
            for t in range(BANDS):
                upper = paired[t // 2][:, pairs, 0, :]
                lower = paired[t // 2][:, pairs, 1, :]
                first, second, combine = (
                    (lower, upper, ALU.subtract) if t % 2 else (upper, lower, ALU.add)
                )
                nc.vector.scalar_tensor_tensor(
                    out=bands[:, t, px].rearrange("p (i j) -> p i j", j=HALF_W),
                    in0=first,
                    scalar=shift[:, t : t + 1],
                    in1=second,
                    op0=ALU.subtract,
                    op1=combine,
                    accum_out=sums[:, half, t : t + 1],
                )
                nc.scalar.activation(
                    out=squares_scrap[:, half, t, :],
                    in_=bands[:, t, px],
                    func=ACT.Square,
                    accum_out=sumsq[:, half, t : t + 1],
                )
            first_half, last_half = half == 0, half == HALVES - 1
            nc.tensor.matmul(
                out=mean_ps[:], lhsT=group_avg_2d, rhs=sums[:, half, :],
                start=first_half, stop=last_half,
            )
            nc.tensor.matmul(
                out=meansq_ps[:], lhsT=group_avg_2d, rhs=sumsq[:, half, :],
                start=first_half, stop=last_half,
            )

        w_codes = keep.tile([P, CO], U32, align_bytes=64)
        w_scales = keep.tile([P, CO], U8, align_bytes=64)
        nc.vector.quantize_mx(
            out=w_codes[:].bitcast(FP8X4),
            scales=w_scales[:],
            in_=w_grouped[:].rearrange("p m o t -> p (m o t)"),
        )

        mean = keep.tile([P, BANDS], F32)
        nc.vector.tensor_copy(out=mean[:], in_=mean_ps[:])
        mean_squared = keep.tile([P, BANDS], F32)
        nc.vector.tensor_tensor(out=mean_squared[:], in0=mean_ps[:], in1=mean[:], op=ALU.mult)
        nc.vector.scalar_tensor_tensor(
            out=gain_pull[:, 1, 0:BANDS],
            in0=mean[:],
            scalar=-1.0,
            in1=gain_pull[:, 0, 0:BANDS],
            op0=ALU.mult,
            op1=ALU.mult,
        )
        var_eps = keep.tile([P, BANDS], F32)
        nc.vector.scalar_tensor_tensor(
            out=var_eps[:],
            in0=meansq_ps[:],
            scalar=EPS_UNHALVED,
            in1=mean_squared[:],
            op0=ALU.add,
            op1=ALU.subtract,
        )
        std = keep.tile([P, BANDS], F32)
        nc.scalar.activation(out=std[:], in_=var_eps[:], func=ACT.Sqrt)
        rstd = keep.tile([P, BANDS], F32)
        nc.vector.reciprocal(out=rstd[:], in_=std[:])
        slope_pull = keep.tile([P, 2, BANDS], F32)
        nc.vector.tensor_tensor(
            out=slope_pull[:],
            in0=gain_pull[:, :, 0:BANDS],
            in1=rstd[:].unsqueeze(1).to_broadcast([P, 2, BANDS]),
            op=ALU.mult,
        )
        offset = keep.tile([P, BANDS], F32)
        nc.vector.tensor_tensor(
            out=offset[:], in0=slope_pull[:, 1, :], in1=gn_bias_sb[:], op=ALU.add
        )

        y_planar = keep.tile([P, BANDS, PIX], BF16)
        for n in range(N_TILES):
            px = slice(n * N_PIX, (n + 1) * N_PIX)
            for t in range(BANDS):
                slope_t, offset_t = slope_pull[:, 0, t : t + 1], offset[:, t : t + 1]
                if t % 2 == 0:
                    nc.scalar.activation(
                        out=y_planar[:, t, px], in_=bands[:, t, px],
                        func=ACT.Identity, scale=slope_t, bias=offset_t,
                    )
                else:
                    nc.vector.tensor_scalar(
                        out=y_planar[:, t, px], in0=bands[:, t, px],
                        scalar1=slope_t, scalar2=offset_t, op0=ALU.mult, op1=ALU.add,
                    )

        y_grouped = keep.tile([P, PIX, BANDS], BF16, align_bytes=64)
        y_codes = keep.tile([P, PIX], U32, align_bytes=64)
        y_scales = keep.tile([P, PIX], U8, align_bytes=64)
        out_dram = out.rearrange("(m o) i j -> m o (i j)", o=P)

        def regroup(n):
            px = slice(n * N_PIX, (n + 1) * N_PIX)
            nc.vector.tensor_copy(
                out=y_grouped[:, px, :].rearrange("p (c r) t -> p c t r", r=RUN),
                in_=y_planar[:, :, px].rearrange("p t (c r) -> p c t r", r=RUN),
            )

        regroup(0)
        for n in range(N_TILES):
            px = slice(n * N_PIX, (n + 1) * N_PIX)
            if n + 1 < N_TILES:
                regroup(n + 1)
            nc.vector.quantize_mx(
                out=y_codes[:, px].bitcast(FP8X4),
                scales=y_scales[:, px],
                in_=y_grouped[:, px, :].rearrange("p c t -> p (c t)"),
            )
            for m in range(M_TILES):
                o_cols = slice(m * P, (m + 1) * P)
                acc = acc_pool.tile([P, N_PIX], F32)
                nc.tensor.matmul_mx(
                    out=acc[:],
                    lhsT=w_codes[:, o_cols].bitcast(FP8X4),
                    lhsT_scale=w_scales[:, o_cols],
                    rhs=y_codes[:, px].bitcast(FP8X4),
                    rhs_scale=y_scales[:, px],
                    start=True,
                    stop=True,
                )
                result = keep.tile([P, N_PIX], F32, name="result%d%d" % (n, m))
                if n == N_TILES - 1 and m == M_TILES - 1:
                    nc.vector.tensor_scalar_max(out=result[:], in0=acc[:], scalar1=0.0)
                else:
                    nc.scalar.activation(out=result[:], in_=acc[:], func=ACT.Relu)
                nc.sync.dma_start(out=out_dram[m][:, px], in_=result[:])
